import numpy as np
import ml_dtypes

BF16 = ml_dtypes.bfloat16


def bf(x):
    return np.asarray(x, np.float32).astype(BF16)


def f32(x):
    return np.asarray(x, np.float32)


def f64(x):
    return np.asarray(x).astype(np.float64)


def striped(idx):
    return np.tile(idx.reshape(-1, 16).T, (8, 1))


B, T, HID, DEP, DS, S, N = 8, 16, 128, 128, 128, 1024, 2048


def setup_inputs():
    sc = 0.5 / np.sqrt(HID + DEP)
    return {
        "table": bf(np.random.standard_normal((DEP, S))),
        "h": bf(np.random.standard_normal((HID, B * T))),
        "w1h": bf(sc * np.random.standard_normal((HID, DS))),
        "w1d": bf(sc * np.random.standard_normal((DEP, DS))),
        "b1": f32(0.1 * np.random.standard_normal((DS, 1))),
        "w2h": bf(sc * np.random.standard_normal((HID, DS))),
        "w2d": bf(sc * np.random.standard_normal((DEP, DS))),
        "b2": f32(0.1 * np.random.standard_normal((DS, 1))),
        "offs": striped(np.random.permutation(np.tile(np.arange(S), 2))[:N]),
    }


def reference(table, h, w1h, w1d, b1, w2h, w2d, b2, offs):
    idx = offs[:16].T.reshape(-1)
    picked = f64(table)[:, idx]
    d1 = (f64(w1d).T @ picked).reshape(DS, B, T, T)
    d2 = (f64(w2d).T @ picked).reshape(DS, B, T, T)
    p1 = (f64(w1h).T @ f64(h) + f64(b1)).reshape(DS, B, T, 1)
    p2 = (f64(w2h).T @ f64(h) + f64(b2)).reshape(DS, B, 1, T)
    u = d1 + p1
    v = d2 + p2
    return (u * v).reshape(DS, N)

@@ -1,0 +1,75 @@
+import concourse.mybir as mybir
+
+BF16, F32, U16 = mybir.dt.bfloat16, mybir.dt.float32, mybir.dt.uint16
+ADD, MULT = mybir.AluOpType.add, mybir.AluOpType.mult
+IDENTITY = mybir.ActivationFunctionType.Identity
+
+P = 128
+TYPES = 1024
+TOKENS = 16
+PAIRS = TOKENS * TOKENS
+N = 2048
+PIECE = 512
+PIECES = N // PIECE
+SENTENCES = PIECE // PAIRS
+FIRSTS = PIECE // TOKENS
+
+FLOPS = 2 * P * P * (2 * N + 2 * P)
+
+
+def tile_typeenhancedgcn_kernel(tc, table, h, w1h, w1d, b1, w2h, w2d, b2, offs, out):
+    nc = tc.nc
+    with (
+        tc.tile_pool(name="held", bufs=1) as held,
+        tc.tile_pool(name="work", bufs=2) as work,
+        tc.psum_pool(name="psum", bufs=1) as psum,
+    ):
+        offsets = held.tile([P, N // 16], U16, name="offsets")
+        nc.sync.dma_start(offsets[:], offs)
+        table_sb = held.tile([P, TYPES], BF16, name="table_sb")
+        nc.sync.dma_start(table_sb[:], table)
+
+        h_sb = held.tile([P, P], BF16, name="h_sb")
+        w1h_sb = held.tile([P, P], BF16, name="w1h_sb")
+        w2h_sb = held.tile([P, P], BF16, name="w2h_sb")
+        w1d_sb = held.tile([P, P], BF16, name="w1d_sb")
+        w2d_sb = held.tile([P, P], BF16, name="w2d_sb")
+        for tile, source in ((h_sb, h), (w1h_sb, w1h), (w2h_sb, w2h), (w1d_sb, w1d), (w2d_sb, w2d)):
+            nc.scalar.dma_start(tile[:], source)
+        b1_sb = held.tile([P, 1], F32, name="b1_sb")
+        b2_sb = held.tile([P, 1], F32, name="b2_sb")
+        nc.gpsimd.dma_start(b1_sb[:], b1)
+        nc.gpsimd.dma_start(b2_sb[:], b2)
+
+        u_ps = [psum.tile([P, PIECE], F32, name=f"u_ps{c}") for c in range(PIECES)]
+        v_ps = [psum.tile([P, PIECE], F32, name=f"v_ps{c}") for c in range(PIECES)]
+
+        for c in range(PIECES):
+            h_piece = h_sb[:, c * FIRSTS : (c + 1) * FIRSTS]
+            first_token = h_piece.unsqueeze(2).to_broadcast([P, FIRSTS, TOKENS])
+            second_token = (
+                h_piece.rearrange("p (s t) -> p s t", t=TOKENS)
+                .unsqueeze(2)
+                .to_broadcast([P, SENTENCES, TOKENS, TOKENS])
+            )
+            nc.tensor.matmul(
+                u_ps[c][:].rearrange("p (f t) -> p f t", t=TOKENS), w1h_sb[:], first_token, start=True, stop=False
+            )
+            nc.tensor.matmul(
+                v_ps[c][:].rearrange("p (s f t) -> p s f t", f=TOKENS, t=TOKENS),
+                w2h_sb[:],
+                second_token,
+                start=True,
+                stop=False,
+            )
+
+        for c in range(PIECES):
+            looked_up = table_sb[:].indirect(offsets[:, c * (PIECE // 16) : (c + 1) * (PIECE // 16)])
+            nc.tensor.matmul(u_ps[c][:], w1d_sb[:], looked_up, start=False, stop=True)
+            nc.tensor.matmul(v_ps[c][:], w2d_sb[:], looked_up, start=False, stop=True)
+
+            u_sb = work.tile([P, PIECE], F32, name="u_sb")
+            nc.scalar.activation(u_sb[:], u_ps[c][:], IDENTITY, bias=b1_sb[:])
+            product = work.tile([P, PIECE], F32, name="product")
+            nc.vector.scalar_tensor_tensor(product[:], v_ps[c][:], b2_sb[:], u_sb[:], ADD, MULT)
+            nc.sync.dma_start(out[:, c * PIECE : (c + 1) * PIECE], product[:])

@@ -21,24 +21,26 @@ def tile_typeenhancedgcn_kernel(tc, table, h, w1h, w1d, b1, w2h, w2d, b2, offs, 
     nc = tc.nc
     with (
         tc.tile_pool(name="held", bufs=1) as held,
-        tc.tile_pool(name="work", bufs=2) as work,
+        tc.tile_pool(name="work", bufs=PIECES) as work,
         tc.psum_pool(name="psum", bufs=1) as psum,
     ):
         offsets = held.tile([P, N // 16], U16, name="offsets")
-        nc.sync.dma_start(offsets[:], offs)
         table_sb = held.tile([P, TYPES], BF16, name="table_sb")
-        nc.sync.dma_start(table_sb[:], table)
-
         h_sb = held.tile([P, P], BF16, name="h_sb")
         w1h_sb = held.tile([P, P], BF16, name="w1h_sb")
         w2h_sb = held.tile([P, P], BF16, name="w2h_sb")
         w1d_sb = held.tile([P, P], BF16, name="w1d_sb")
         w2d_sb = held.tile([P, P], BF16, name="w2d_sb")
-        for tile, source in ((h_sb, h), (w1h_sb, w1h), (w2h_sb, w2h), (w1d_sb, w1d), (w2d_sb, w2d)):
-            nc.scalar.dma_start(tile[:], source)
         b1_sb = held.tile([P, 1], F32, name="b1_sb")
         b2_sb = held.tile([P, 1], F32, name="b2_sb")
-        nc.gpsimd.dma_start(b1_sb[:], b1)
+        nc.sync.dma_start(h_sb[:], h)
+        nc.scalar.dma_start(w1h_sb[:], w1h)
+        nc.scalar.dma_start(w2h_sb[:], w2h)
+        nc.sync.dma_start(offsets[:], offs)
+        nc.sync.dma_start(table_sb[:], table)
+        nc.scalar.dma_start(w1d_sb[:], w1d)
+        nc.scalar.dma_start(w2d_sb[:], w2d)
+        nc.sync.dma_start(b1_sb[:], b1)
         nc.gpsimd.dma_start(b2_sb[:], b2)
 
         u_ps = [psum.tile([P, PIECE], F32, name=f"u_ps{c}") for c in range(PIECES)]

@@ -14,6 +14,8 @@ PIECES = N // PIECE
 SENTENCES = PIECE // PAIRS
 FIRSTS = PIECE // TOKENS
 
+WARM_UP = 5
+
 FLOPS = 2 * P * P * (2 * N + 2 * P)
 
 
@@ -45,6 +47,11 @@ def tile_typeenhancedgcn_kernel(tc, table, h, w1h, w1d, b1, w2h, w2d, b2, offs, 
 
         u_ps = [psum.tile([P, PIECE], F32, name=f"u_ps{c}") for c in range(PIECES)]
         v_ps = [psum.tile([P, PIECE], F32, name=f"v_ps{c}") for c in range(PIECES)]
+
+        zeros = held.tile([P, PIECE], BF16, name="zeros")
+        nc.vector.memset(zeros[:], 0.0)
+        for turn in range(WARM_UP):
+            nc.tensor.matmul(v_ps[PIECES - 1][:], zeros[:, 0:P], zeros[:], start=True, stop=True)
 
         for c in range(PIECES):
             h_piece = h_sb[:, c * FIRSTS : (c + 1) * FIRSTS]

@@ -14,7 +14,7 @@ PIECES = N // PIECE
 SENTENCES = PIECE // PAIRS
 FIRSTS = PIECE // TOKENS
 
-WARM_UP = 5
+WARM_UP = 3
 
 FLOPS = 2 * P * P * (2 * N + 2 * P)
 
@@ -35,6 +35,8 @@ def tile_typeenhancedgcn_kernel(tc, table, h, w1h, w1d, b1, w2h, w2d, b2, offs, 
         w2d_sb = held.tile([P, P], BF16, name="w2d_sb")
         b1_sb = held.tile([P, 1], F32, name="b1_sb")
         b2_sb = held.tile([P, 1], F32, name="b2_sb")
+        zeros = held.tile([P, P], BF16, name="zeros")
+        nc.gpsimd.memset(zeros[:], 0.0)
         nc.sync.dma_start(h_sb[:], h)
         nc.scalar.dma_start(w1h_sb[:], w1h)
         nc.scalar.dma_start(w2h_sb[:], w2h)
@@ -48,10 +50,14 @@ def tile_typeenhancedgcn_kernel(tc, table, h, w1h, w1d, b1, w2h, w2d, b2, offs, 
         u_ps = [psum.tile([P, PIECE], F32, name=f"u_ps{c}") for c in range(PIECES)]
         v_ps = [psum.tile([P, PIECE], F32, name=f"v_ps{c}") for c in range(PIECES)]
 
-        zeros = held.tile([P, PIECE], BF16, name="zeros")
-        nc.vector.memset(zeros[:], 0.0)
         for turn in range(WARM_UP):
-            nc.tensor.matmul(v_ps[PIECES - 1][:], zeros[:, 0:P], zeros[:], start=True, stop=True)
+            nc.tensor.matmul(
+                v_ps[PIECES - 1][:].rearrange("p (r z) -> p r z", z=P),
+                zeros[:],
+                zeros[:].unsqueeze(1).to_broadcast([P, PIECE // P, P]),
+                start=True,
+                stop=True,
+            )
 
         for c in range(PIECES):
             h_piece = h_sb[:, c * FIRSTS : (c + 1) * FIRSTS]
@@ -72,13 +78,23 @@ def tile_typeenhancedgcn_kernel(tc, table, h, w1h, w1d, b1, w2h, w2d, b2, offs, 
                 stop=False,
             )
 
-        for c in range(PIECES):
-            looked_up = table_sb[:].indirect(offsets[:, c * (PIECE // 16) : (c + 1) * (PIECE // 16)])
-            nc.tensor.matmul(u_ps[c][:], w1d_sb[:], looked_up, start=False, stop=True)
-            nc.tensor.matmul(v_ps[c][:], w2d_sb[:], looked_up, start=False, stop=True)
+        def looked_up(c):
+            return table_sb[:].indirect(offsets[:, c * (PIECE // 16) : (c + 1) * (PIECE // 16)])
 
-            u_sb = work.tile([P, PIECE], F32, name="u_sb")
-            nc.scalar.activation(u_sb[:], u_ps[c][:], IDENTITY, bias=b1_sb[:])
+        u_sb = [held.tile([P, PIECE], F32, name=f"u_sb{c}") for c in range(PIECES)]
+
+        def close_u(c):
+            nc.tensor.matmul(u_ps[c][:], w1d_sb[:], looked_up(c), start=False, stop=True)
+            nc.scalar.activation(u_sb[c][:], u_ps[c][:], IDENTITY, bias=b1_sb[:])
+
+        def close_v(c):
+            nc.tensor.matmul(v_ps[c][:], w2d_sb[:], looked_up(c), start=False, stop=True)
             product = work.tile([P, PIECE], F32, name="product")
-            nc.vector.scalar_tensor_tensor(product[:], v_ps[c][:], b2_sb[:], u_sb[:], ADD, MULT)
+            nc.vector.scalar_tensor_tensor(product[:], v_ps[c][:], b2_sb[:], u_sb[c][:], ADD, MULT)
             nc.sync.dma_start(out[:, c * PIECE : (c + 1) * PIECE], product[:])
+
+        close_u(0)
+        for c in range(1, PIECES):
+            close_u(c)
+            close_v(c - 1)
+        close_v(PIECES - 1)

@@ -45,7 +45,7 @@ def tile_typeenhancedgcn_kernel(tc, table, h, w1h, w1d, b1, w2h, w2d, b2, offs, 
         nc.scalar.dma_start(w1d_sb[:], w1d)
         nc.scalar.dma_start(w2d_sb[:], w2d)
         nc.sync.dma_start(b1_sb[:], b1)
-        nc.gpsimd.dma_start(b2_sb[:], b2)
+        nc.sync.dma_start(b2_sb[:], b2)
 
         u_ps = [psum.tile([P, PIECE], F32, name=f"u_ps{c}") for c in range(PIECES)]
         v_ps = [psum.tile([P, PIECE], F32, name=f"v_ps{c}") for c in range(PIECES)]

@@ -2,7 +2,6 @@ import concourse.mybir as mybir
 
 BF16, F32, U16 = mybir.dt.bfloat16, mybir.dt.float32, mybir.dt.uint16
 ADD, MULT = mybir.AluOpType.add, mybir.AluOpType.mult
-IDENTITY = mybir.ActivationFunctionType.Identity
 
 P = 128
 TYPES = 1024
@@ -38,13 +37,13 @@ def tile_typeenhancedgcn_kernel(tc, table, h, w1h, w1d, b1, w2h, w2d, b2, offs, 
         zeros = held.tile([P, P], BF16, name="zeros")
         nc.gpsimd.memset(zeros[:], 0.0)
         nc.sync.dma_start(h_sb[:], h)
-        nc.scalar.dma_start(w1h_sb[:], w1h)
-        nc.scalar.dma_start(w2h_sb[:], w2h)
+        nc.sync.dma_start(w1h_sb[:], w1h)
+        nc.sync.dma_start(w2h_sb[:], w2h)
+        nc.sync.dma_start(b1_sb[:], b1)
         nc.sync.dma_start(offsets[:], offs)
         nc.sync.dma_start(table_sb[:], table)
-        nc.scalar.dma_start(w1d_sb[:], w1d)
-        nc.scalar.dma_start(w2d_sb[:], w2d)
-        nc.sync.dma_start(b1_sb[:], b1)
+        nc.sync.dma_start(w1d_sb[:], w1d)
+        nc.sync.dma_start(w2d_sb[:], w2d)
         nc.sync.dma_start(b2_sb[:], b2)
 
         u_ps = [psum.tile([P, PIECE], F32, name=f"u_ps{c}") for c in range(PIECES)]
@@ -59,16 +58,16 @@ def tile_typeenhancedgcn_kernel(tc, table, h, w1h, w1d, b1, w2h, w2d, b2, offs, 
                 stop=True,
             )
 
+        nc.tensor.matmul(u_ps[0][:, 0:P], w1h_sb[:], h_sb[:], start=True, stop=True)
+        first_term = held.tile([P, P], F32, name="first_term")
+        nc.vector.tensor_scalar_add(first_term[:], u_ps[0][:, 0:P], b1_sb[:])
+
         for c in range(PIECES):
-            h_piece = h_sb[:, c * FIRSTS : (c + 1) * FIRSTS]
-            first_token = h_piece.unsqueeze(2).to_broadcast([P, FIRSTS, TOKENS])
             second_token = (
-                h_piece.rearrange("p (s t) -> p s t", t=TOKENS)
+                h_sb[:, c * FIRSTS : (c + 1) * FIRSTS]
+                .rearrange("p (s t) -> p s t", t=TOKENS)
                 .unsqueeze(2)
                 .to_broadcast([P, SENTENCES, TOKENS, TOKENS])
-            )
-            nc.tensor.matmul(
-                u_ps[c][:].rearrange("p (f t) -> p f t", t=TOKENS), w1h_sb[:], first_token, start=True, stop=False
             )
             nc.tensor.matmul(
                 v_ps[c][:].rearrange("p (s f t) -> p s f t", f=TOKENS, t=TOKENS),
@@ -83,9 +82,14 @@ def tile_typeenhancedgcn_kernel(tc, table, h, w1h, w1d, b1, w2h, w2d, b2, offs, 
 
         u_sb = [held.tile([P, PIECE], F32, name=f"u_sb{c}") for c in range(PIECES)]
 
-        def close_u(c):
-            nc.tensor.matmul(u_ps[c][:], w1d_sb[:], looked_up(c), start=False, stop=True)
-            nc.scalar.activation(u_sb[c][:], u_ps[c][:], IDENTITY, bias=b1_sb[:])
+        def make_u(c):
+            nc.tensor.matmul(u_ps[c][:], w1d_sb[:], looked_up(c), start=True, stop=True)
+            nc.vector.tensor_tensor(
+                u_sb[c][:].rearrange("p (f t) -> p f t", t=TOKENS),
+                u_ps[c][:].rearrange("p (f t) -> p f t", t=TOKENS),
+                first_term[:, c * FIRSTS : (c + 1) * FIRSTS].unsqueeze(2).to_broadcast([P, FIRSTS, TOKENS]),
+                ADD,
+            )
 
         def close_v(c):
             nc.tensor.matmul(v_ps[c][:], w2d_sb[:], looked_up(c), start=False, stop=True)
@@ -93,8 +97,8 @@ def tile_typeenhancedgcn_kernel(tc, table, h, w1h, w1d, b1, w2h, w2d, b2, offs, 
             nc.vector.scalar_tensor_tensor(product[:], v_ps[c][:], b2_sb[:], u_sb[c][:], ADD, MULT)
             nc.sync.dma_start(out[:, c * PIECE : (c + 1) * PIECE], product[:])
 
-        close_u(0)
+        make_u(0)
         for c in range(1, PIECES):
-            close_u(c)
+            make_u(c)
             close_v(c - 1)
         close_v(PIECES - 1)

@@ -39,11 +39,11 @@ def tile_typeenhancedgcn_kernel(tc, table, h, w1h, w1d, b1, w2h, w2d, b2, offs, 
         nc.sync.dma_start(h_sb[:], h)
         nc.sync.dma_start(w1h_sb[:], w1h)
         nc.sync.dma_start(w2h_sb[:], w2h)
-        nc.sync.dma_start(b1_sb[:], b1)
-        nc.sync.dma_start(offsets[:], offs)
-        nc.sync.dma_start(table_sb[:], table)
         nc.sync.dma_start(w1d_sb[:], w1d)
         nc.sync.dma_start(w2d_sb[:], w2d)
+        nc.sync.dma_start(offsets[:], offs)
+        nc.sync.dma_start(table_sb[:], table)
+        nc.sync.dma_start(b1_sb[:], b1)
         nc.sync.dma_start(b2_sb[:], b2)
 
         u_ps = [psum.tile([P, PIECE], F32, name=f"u_ps{c}") for c in range(PIECES)]
@@ -60,7 +60,7 @@ def tile_typeenhancedgcn_kernel(tc, table, h, w1h, w1d, b1, w2h, w2d, b2, offs, 
 
         nc.tensor.matmul(u_ps[0][:, 0:P], w1h_sb[:], h_sb[:], start=True, stop=True)
         first_term = held.tile([P, P], F32, name="first_term")
-        nc.vector.tensor_scalar_add(first_term[:], u_ps[0][:, 0:P], b1_sb[:])
+        nc.vector.tensor_copy(first_term[:], u_ps[0][:, 0:P])
 
         for c in range(PIECES):
             second_token = (
@@ -84,10 +84,12 @@ def tile_typeenhancedgcn_kernel(tc, table, h, w1h, w1d, b1, w2h, w2d, b2, offs, 
 
         def make_u(c):
             nc.tensor.matmul(u_ps[c][:], w1d_sb[:], looked_up(c), start=True, stop=True)
-            nc.vector.tensor_tensor(
+            nc.vector.scalar_tensor_tensor(
                 u_sb[c][:].rearrange("p (f t) -> p f t", t=TOKENS),
                 u_ps[c][:].rearrange("p (f t) -> p f t", t=TOKENS),
+                b1_sb[:],
                 first_term[:, c * FIRSTS : (c + 1) * FIRSTS].unsqueeze(2).to_broadcast([P, FIRSTS, TOKENS]),
+                ADD,
                 ADD,
             )
 

@@ -96,8 +96,12 @@ def tile_typeenhancedgcn_kernel(tc, table, h, w1h, w1d, b1, w2h, w2d, b2, offs, 
         def close_v(c):
             nc.tensor.matmul(v_ps[c][:], w2d_sb[:], looked_up(c), start=False, stop=True)
             product = work.tile([P, PIECE], F32, name="product")
-            nc.vector.scalar_tensor_tensor(product[:], v_ps[c][:], b2_sb[:], u_sb[c][:], ADD, MULT)
-            nc.sync.dma_start(out[:, c * PIECE : (c + 1) * PIECE], product[:])
+            cuts = 2 if c == PIECES - 1 else 1
+            width = PIECE // cuts
+            for k in range(cuts):
+                a, b = k * width, (k + 1) * width
+                nc.vector.scalar_tensor_tensor(product[:, a:b], v_ps[c][:, a:b], b2_sb[:], u_sb[c][:, a:b], ADD, MULT)
+                nc.sync.dma_start(out[:, c * PIECE + a : c * PIECE + b], product[:, a:b])
 
         make_u(0)
         for c in range(1, PIECES):

@@ -96,7 +96,7 @@ def tile_typeenhancedgcn_kernel(tc, table, h, w1h, w1d, b1, w2h, w2d, b2, offs, 
         def close_v(c):
             nc.tensor.matmul(v_ps[c][:], w2d_sb[:], looked_up(c), start=False, stop=True)
             product = work.tile([P, PIECE], F32, name="product")
-            cuts = 2 if c == PIECES - 1 else 1
+            cuts = 2 if c >= PIECES - 2 else 1
             width = PIECE // cuts
             for k in range(cuts):
                 a, b = k * width, (k + 1) * width

@@ -37,12 +37,12 @@ def tile_typeenhancedgcn_kernel(tc, table, h, w1h, w1d, b1, w2h, w2d, b2, offs, 
         zeros = held.tile([P, P], BF16, name="zeros")
         nc.gpsimd.memset(zeros[:], 0.0)
         nc.sync.dma_start(h_sb[:], h)
-        nc.sync.dma_start(w1h_sb[:], w1h)
         nc.sync.dma_start(w2h_sb[:], w2h)
+        nc.sync.dma_start(w1h_sb[:], w1h)
+        nc.sync.dma_start(table_sb[:], table)
         nc.sync.dma_start(w1d_sb[:], w1d)
         nc.sync.dma_start(w2d_sb[:], w2d)
         nc.sync.dma_start(offsets[:], offs)
-        nc.sync.dma_start(table_sb[:], table)
         nc.sync.dma_start(b1_sb[:], b1)
         nc.sync.dma_start(b2_sb[:], b2)
 
@@ -58,9 +58,9 @@ def tile_typeenhancedgcn_kernel(tc, table, h, w1h, w1d, b1, w2h, w2d, b2, offs, 
                 stop=True,
             )
 
-        nc.tensor.matmul(u_ps[0][:, 0:P], w1h_sb[:], h_sb[:], start=True, stop=True)
+        nc.tensor.matmul(u_ps[PIECES - 1][:, 0:P], w1h_sb[:], h_sb[:], start=True, stop=True)
         first_term = held.tile([P, P], F32, name="first_term")
-        nc.vector.tensor_copy(first_term[:], u_ps[0][:, 0:P])
+        nc.vector.tensor_copy(first_term[:], u_ps[PIECES - 1][:, 0:P])
 
         for c in range(PIECES):
             second_token = (

@@ -60,7 +60,7 @@ def tile_typeenhancedgcn_kernel(tc, table, h, w1h, w1d, b1, w2h, w2d, b2, offs, 
 
         nc.tensor.matmul(u_ps[PIECES - 1][:, 0:P], w1h_sb[:], h_sb[:], start=True, stop=True)
         first_term = held.tile([P, P], F32, name="first_term")
-        nc.vector.tensor_copy(first_term[:], u_ps[PIECES - 1][:, 0:P])
+        nc.vector.tensor_scalar_add(first_term[:], u_ps[PIECES - 1][:, 0:P], b1_sb[:])
 
         for c in range(PIECES):
             second_token = (
@@ -84,12 +84,10 @@ def tile_typeenhancedgcn_kernel(tc, table, h, w1h, w1d, b1, w2h, w2d, b2, offs, 
 
         def make_u(c):
             nc.tensor.matmul(u_ps[c][:], w1d_sb[:], looked_up(c), start=True, stop=True)
-            nc.vector.scalar_tensor_tensor(
+            nc.vector.tensor_tensor(
                 u_sb[c][:].rearrange("p (f t) -> p f t", t=TOKENS),
                 u_ps[c][:].rearrange("p (f t) -> p f t", t=TOKENS),
-                b1_sb[:],
                 first_term[:, c * FIRSTS : (c + 1) * FIRSTS].unsqueeze(2).to_broadcast([P, FIRSTS, TOKENS]),
-                ADD,
                 ADD,
             )
 

@@ -2,6 +2,7 @@ import concourse.mybir as mybir
 
 BF16, F32, U16 = mybir.dt.bfloat16, mybir.dt.float32, mybir.dt.uint16
 ADD, MULT = mybir.AluOpType.add, mybir.AluOpType.mult
+IDENTITY = mybir.ActivationFunctionType.Identity
 
 P = 128
 TYPES = 1024
@@ -58,11 +59,17 @@ def tile_typeenhancedgcn_kernel(tc, table, h, w1h, w1d, b1, w2h, w2d, b2, offs, 
                 stop=True,
             )
 
-        nc.tensor.matmul(u_ps[PIECES - 1][:, 0:P], w1h_sb[:], h_sb[:], start=True, stop=True)
-        first_term = held.tile([P, P], F32, name="first_term")
-        nc.vector.tensor_scalar_add(first_term[:], u_ps[PIECES - 1][:, 0:P], b1_sb[:])
+        borrowed = u_ps[PIECES - 2]
+        nc.tensor.matmul(borrowed[:, 0:P], w1h_sb[:], h_sb[:], start=True, stop=True)
+        nc.tensor.matmul(borrowed[:, P : P + FIRSTS], w2h_sb[:], h_sb[:, 0:FIRSTS], start=True, stop=True)
+        terms = held.tile([P, P + FIRSTS], F32, name="terms")
+        nc.vector.tensor_copy(terms[:], borrowed[:, 0 : P + FIRSTS])
+        first_term = terms[:, 0:P]
+        second_term = terms[:, P : P + FIRSTS]
+        last_bias = held.tile([P, FIRSTS], F32, name="last_bias")
+        nc.scalar.activation(last_bias[:], first_term[:, (PIECES - 1) * FIRSTS : P], IDENTITY, bias=b1_sb[:])
 
-        for c in range(PIECES):
+        for c in range(1, PIECES):
             second_token = (
                 h_sb[:, c * FIRSTS : (c + 1) * FIRSTS]
                 .rearrange("p (s t) -> p s t", t=TOKENS)
@@ -82,27 +89,67 @@ def tile_typeenhancedgcn_kernel(tc, table, h, w1h, w1d, b1, w2h, w2d, b2, offs, 
 
         u_sb = [held.tile([P, PIECE], F32, name=f"u_sb{c}") for c in range(PIECES)]
 
-        def make_u(c):
+        def gather_u(c):
             nc.tensor.matmul(u_ps[c][:], w1d_sb[:], looked_up(c), start=True, stop=True)
-            nc.vector.tensor_tensor(
+
+        def u_by_vector(c):
+            gather_u(c)
+            nc.vector.scalar_tensor_tensor(
                 u_sb[c][:].rearrange("p (f t) -> p f t", t=TOKENS),
                 u_ps[c][:].rearrange("p (f t) -> p f t", t=TOKENS),
+                b1_sb[:],
                 first_term[:, c * FIRSTS : (c + 1) * FIRSTS].unsqueeze(2).to_broadcast([P, FIRSTS, TOKENS]),
                 ADD,
+                ADD,
             )
+
+        def u_by_scalar(c):
+            gather_u(c)
+            for f in range(FIRSTS):
+                nc.scalar.activation(
+                    u_sb[c][:, f * TOKENS : (f + 1) * TOKENS],
+                    u_ps[c][:, f * TOKENS : (f + 1) * TOKENS],
+                    IDENTITY,
+                    bias=last_bias[:, f : f + 1],
+                )
+
+        def store(c, product, a, b):
+            nc.sync.dma_start(out[:, c * PIECE + a : c * PIECE + b], product[:, a:b])
+
+        v_sb = held.tile([P, PIECE], F32, name="v_sb")
+
+        def first_piece_v():
+            nc.tensor.matmul(v_ps[0][:], w2d_sb[:], looked_up(0), start=True, stop=True)
+            nc.vector.tensor_tensor(
+                v_sb[:].rearrange("p (s f t) -> p s f t", f=TOKENS, t=TOKENS),
+                v_ps[0][:].rearrange("p (s f t) -> p s f t", f=TOKENS, t=TOKENS),
+                second_term.rearrange("p (s t) -> p s t", t=TOKENS)
+                .unsqueeze(2)
+                .to_broadcast([P, SENTENCES, TOKENS, TOKENS]),
+                ADD,
+            )
+
+        def first_piece_product():
+            product = work.tile([P, PIECE], F32, name="product")
+            nc.vector.scalar_tensor_tensor(product[:], v_sb[:], b2_sb[:], u_sb[0][:], ADD, MULT)
+            store(0, product, 0, PIECE)
 
         def close_v(c):
             nc.tensor.matmul(v_ps[c][:], w2d_sb[:], looked_up(c), start=False, stop=True)
             product = work.tile([P, PIECE], F32, name="product")
-            cuts = 2 if c >= PIECES - 2 else 1
+            cuts = 2
             width = PIECE // cuts
             for k in range(cuts):
                 a, b = k * width, (k + 1) * width
                 nc.vector.scalar_tensor_tensor(product[:, a:b], v_ps[c][:, a:b], b2_sb[:], u_sb[c][:, a:b], ADD, MULT)
-                nc.sync.dma_start(out[:, c * PIECE + a : c * PIECE + b], product[:, a:b])
+                store(c, product, a, b)
 
-        make_u(0)
-        for c in range(1, PIECES):
-            make_u(c)
-            close_v(c - 1)
-        close_v(PIECES - 1)
+        first_piece_v()
+        u_by_vector(0)
+        u_by_vector(1)
+        first_piece_product()
+        u_by_scalar(PIECES - 1)
+        u_by_vector(2)
+        close_v(1)
+        close_v(2)
+        close_v(3)

import concourse.mybir as mybir

BF16, F32, U16 = mybir.dt.bfloat16, mybir.dt.float32, mybir.dt.uint16
ADD, MULT = mybir.AluOpType.add, mybir.AluOpType.mult
IDENTITY = mybir.ActivationFunctionType.Identity

P = 128
TYPES = 1024
TOKENS = 16
PAIRS = TOKENS * TOKENS
N = 2048
PIECE = 512
PIECES = N // PIECE
SENTENCES = PIECE // PAIRS
FIRSTS = PIECE // TOKENS

WARM_UP = 3

FLOPS = 2 * P * P * (2 * N + 2 * P)


def tile_typeenhancedgcn_kernel(tc, table, h, w1h, w1d, b1, w2h, w2d, b2, offs, out):
    nc = tc.nc
    with (
        tc.tile_pool(name="held", bufs=1) as held,
        tc.tile_pool(name="work", bufs=PIECES) as work,
        tc.psum_pool(name="psum", bufs=1) as psum,
    ):
        offsets = held.tile([P, N // 16], U16, name="offsets")
        table_sb = held.tile([P, TYPES], BF16, name="table_sb")
        h_sb = held.tile([P, P], BF16, name="h_sb")
        w1h_sb = held.tile([P, P], BF16, name="w1h_sb")
        w2h_sb = held.tile([P, P], BF16, name="w2h_sb")
        w1d_sb = held.tile([P, P], BF16, name="w1d_sb")
        w2d_sb = held.tile([P, P], BF16, name="w2d_sb")
        b1_sb = held.tile([P, 1], F32, name="b1_sb")
        b2_sb = held.tile([P, 1], F32, name="b2_sb")
        zeros = held.tile([P, P], BF16, name="zeros")
        nc.gpsimd.memset(zeros[:], 0.0)
        nc.sync.dma_start(h_sb[:], h)
        nc.sync.dma_start(w2h_sb[:], w2h)
        nc.sync.dma_start(w1h_sb[:], w1h)
        nc.sync.dma_start(table_sb[:], table)
        nc.sync.dma_start(w1d_sb[:], w1d)
        nc.sync.dma_start(w2d_sb[:], w2d)
        nc.sync.dma_start(offsets[:], offs)
        nc.sync.dma_start(b1_sb[:], b1)
        nc.sync.dma_start(b2_sb[:], b2)

        u_ps = [psum.tile([P, PIECE], F32, name=f"u_ps{c}") for c in range(PIECES)]
        v_ps = [psum.tile([P, PIECE], F32, name=f"v_ps{c}") for c in range(PIECES)]

        for turn in range(WARM_UP):
            nc.tensor.matmul(
                v_ps[PIECES - 1][:].rearrange("p (r z) -> p r z", z=P),
                zeros[:],
                zeros[:].unsqueeze(1).to_broadcast([P, PIECE // P, P]),
                start=True,
                stop=True,
            )

        borrowed = u_ps[PIECES - 2]
        nc.tensor.matmul(borrowed[:, 0:P], w1h_sb[:], h_sb[:], start=True, stop=True)
        nc.tensor.matmul(borrowed[:, P : P + FIRSTS], w2h_sb[:], h_sb[:, 0:FIRSTS], start=True, stop=True)
        terms = held.tile([P, P + FIRSTS], F32, name="terms")
        nc.vector.tensor_copy(terms[:], borrowed[:, 0 : P + FIRSTS])
        first_term = terms[:, 0:P]
        second_term = terms[:, P : P + FIRSTS]
        last_bias = held.tile([P, FIRSTS], F32, name="last_bias")
        nc.scalar.activation(last_bias[:], first_term[:, (PIECES - 1) * FIRSTS : P], IDENTITY, bias=b1_sb[:])

        for c in range(1, PIECES):
            second_token = (
                h_sb[:, c * FIRSTS : (c + 1) * FIRSTS]
                .rearrange("p (s t) -> p s t", t=TOKENS)
                .unsqueeze(2)
                .to_broadcast([P, SENTENCES, TOKENS, TOKENS])
            )
            nc.tensor.matmul(
                v_ps[c][:].rearrange("p (s f t) -> p s f t", f=TOKENS, t=TOKENS),
                w2h_sb[:],
                second_token,
                start=True,
                stop=False,
            )

        def looked_up(c):
            return table_sb[:].indirect(offsets[:, c * (PIECE // 16) : (c + 1) * (PIECE // 16)])

        u_sb = [held.tile([P, PIECE], F32, name=f"u_sb{c}") for c in range(PIECES)]

        def gather_u(c):
            nc.tensor.matmul(u_ps[c][:], w1d_sb[:], looked_up(c), start=True, stop=True)

        def u_by_vector(c):
            gather_u(c)
            nc.vector.scalar_tensor_tensor(
                u_sb[c][:].rearrange("p (f t) -> p f t", t=TOKENS),
                u_ps[c][:].rearrange("p (f t) -> p f t", t=TOKENS),
                b1_sb[:],
                first_term[:, c * FIRSTS : (c + 1) * FIRSTS].unsqueeze(2).to_broadcast([P, FIRSTS, TOKENS]),
                ADD,
                ADD,
            )

        def u_by_scalar(c):
            gather_u(c)
            for f in range(FIRSTS):
                nc.scalar.activation(
                    u_sb[c][:, f * TOKENS : (f + 1) * TOKENS],
                    u_ps[c][:, f * TOKENS : (f + 1) * TOKENS],
                    IDENTITY,
                    bias=last_bias[:, f : f + 1],
                )

        def store(c, product, a, b):
            nc.sync.dma_start(out[:, c * PIECE + a : c * PIECE + b], product[:, a:b])

        v_sb = held.tile([P, PIECE], F32, name="v_sb")

        def first_piece_v():
            nc.tensor.matmul(v_ps[0][:], w2d_sb[:], looked_up(0), start=True, stop=True)
            nc.vector.tensor_tensor(
                v_sb[:].rearrange("p (s f t) -> p s f t", f=TOKENS, t=TOKENS),
                v_ps[0][:].rearrange("p (s f t) -> p s f t", f=TOKENS, t=TOKENS),
                second_term.rearrange("p (s t) -> p s t", t=TOKENS)
                .unsqueeze(2)
                .to_broadcast([P, SENTENCES, TOKENS, TOKENS]),
                ADD,
            )

        def first_piece_product():
            product = work.tile([P, PIECE], F32, name="product")
            nc.vector.scalar_tensor_tensor(product[:], v_sb[:], b2_sb[:], u_sb[0][:], ADD, MULT)
            store(0, product, 0, PIECE)

        def close_v(c):
            nc.tensor.matmul(v_ps[c][:], w2d_sb[:], looked_up(c), start=False, stop=True)
            product = work.tile([P, PIECE], F32, name="product")
            cuts = 2
            width = PIECE // cuts
            for k in range(cuts):
                a, b = k * width, (k + 1) * width
                nc.vector.scalar_tensor_tensor(product[:, a:b], v_ps[c][:, a:b], b2_sb[:], u_sb[c][:, a:b], ADD, MULT)
                store(c, product, a, b)

        first_piece_v()
        u_by_vector(0)
        u_by_vector(1)
        first_piece_product()
        u_by_scalar(PIECES - 1)
        u_by_vector(2)
        close_v(1)
        close_v(2)
        close_v(3)
